import numpy as np
import ml_dtypes


def mxq(x, axis, fmt="e4m3"):
    dtype, down = {"e4m3": (ml_dtypes.float8_e4m3fn, 7), "e5m2": (ml_dtypes.float8_e5m2, 14)}[fmt]
    v = np.moveaxis(np.asarray(x, np.float32).astype(ml_dtypes.bfloat16).astype(np.float64), axis, -1)
    blocks = v.reshape(v.shape[:-1] + (-1, 32))
    amax = np.abs(blocks).max(-1, keepdims=True)
    byte = np.maximum(np.where(amax > 0, np.frexp(amax)[1] - 1 + 127, 0) - down, 1)
    scale = np.exp2(byte - 127.0)
    codes = (blocks / scale).astype(np.float32).astype(dtype).astype(np.float64)
    return np.moveaxis((codes * scale).reshape(v.shape), -1, axis)


WIDE = False


def mx_kscale(k):
    if not WIDE:
        return np.ones(k)
    levels = np.array([10, -10, 5, -5, 0])
    a = np.random.permutation(np.resize(levels, k // 512 * 4)).reshape(k // 512, 4)
    idx = np.arange(k)
    return np.exp2(a[idx // 512, idx % 128 // 32])


BF16 = ml_dtypes.bfloat16


def bf(x):
    return np.asarray(x, np.float32).astype(BF16)


def f64(x):
    return np.asarray(x).astype(np.float64)


E2M1 = np.array([0.0, 0.5, 1.0, 1.5, 2.0, 3.0, 4.0, 6.0, -0.0, -0.5, -1.0, -1.5, -2.0, -3.0, -4.0, -6.0])


def pack_weight(w, fmt):
    k, n = w.shape
    w = f64(bf(w)).reshape(k // 32, 32, n)
    amax = np.abs(w).max(1)
    if fmt == "e4m3":
        byte = np.frexp(amax)[1] - 1 + 127 - 7
    else:
        mant, ex = np.frexp(amax / 6.0)
        byte = np.where(mant > 0.5, ex, ex - 1) + 127
    byte = np.clip(np.where(amax > 0, byte, 1), 1, 254)
    scaled = (w * np.exp2(127.0 - byte)[:, None, :]).reshape(k, n).astype(np.float32)
    by_word = np.ascontiguousarray(scaled.reshape(k // 512, 128, 4, n).transpose(0, 1, 3, 2))
    if fmt == "e4m3":
        words = by_word.astype(ml_dtypes.float8_e4m3fn).view(np.uint8)
    else:
        c = by_word.astype(ml_dtypes.float4_e2m1fn).view(np.uint8) & 0xF
        words = c[..., 0::2] | (c[..., 1::2] << 4)
    return np.ascontiguousarray(words), np.ascontiguousarray(byte.astype(np.uint8).reshape(k // 512, 16, n))


def unpack_weight(words, scales, fmt):
    g, p, n, _ = words.shape
    if fmt == "e4m3":
        vals = np.ascontiguousarray(words).view(ml_dtypes.float8_e4m3fn).astype(np.float64)
    else:
        nib = np.empty((g, p, n, 4), np.uint8)
        nib[..., 0::2] = words & 0xF
        nib[..., 1::2] = words >> 4
        vals = E2M1[nib]
    vals = vals * np.repeat(np.exp2(scales.astype(np.float64) - 127.0), 8, axis=1)[..., None]
    return vals.transpose(0, 1, 3, 2).reshape(g * 512, n)

def pack4(w):
    words, scales = pack_weight(w, "e2m1")
    return words.reshape(words.shape[0], 128, -1), scales


def unpack4(words, scales):
    return unpack_weight(words.reshape(words.shape[0], 128, -1, 2), scales, "e2m1")


N, P, D, E, F = 1024, 3, 512, 1024, 1024
BN_EPS = 1e-5


def setup_inputs():
    t = mx_kscale(E)
    h = 1.2 * np.random.standard_normal((N, P, E)) + 0.6 * np.random.standard_normal((1, P, E))
    w1b_words, w1b_scales = pack4(np.random.standard_normal((E, F)) / np.sqrt(E) / t[:, None])
    w2b_words, w2b_scales = pack4(np.random.standard_normal((E, F)) / np.sqrt(E) / t[:, None])
    return {"h_sage": bf(h * t),
            "w1b_words": w1b_words,
            "w1b_scales": w1b_scales,
            "w2b_words": w2b_words,
            "w2b_scales": w2b_scales,
            "gamma": bf(1.0 + 0.2 * np.random.standard_normal(F)),
            "beta": bf(0.3 * np.random.standard_normal(F))}


def reference(h_sage, w1b_words, w1b_scales, w2b_words, w2b_scales, gamma, beta):
    h = f64(h_sage)
    neigh = (h.sum(axis=1, keepdims=True) - h) * 0.5
    out = (mxq(h[:, 0, :], 1, "e4m3") @ unpack4(w2b_words, w2b_scales)) + (mxq(neigh[:, 0, :], 1, "e4m3") @ unpack4(w1b_words, w1b_scales))
    mean = out.mean(axis=0)
    var = out.var(axis=0)
    out = (out - mean) / np.sqrt(var + BN_EPS) * f64(gamma) + f64(beta)
    return 1.0 / (1.0 + np.exp(-out))

@@ -1,0 +1,256 @@
+from contextlib import ExitStack
+
+import concourse.mybir as mybir
+from concourse.masks import make_identity
+
+F32 = mybir.dt.float32
+BF16 = mybir.dt.bfloat16
+U8 = mybir.dt.uint8
+U32 = mybir.dt.uint32
+I32 = mybir.dt.int32
+FP8X4 = mybir.dt.float8_e4m3fn_x4
+FP4X4 = mybir.dt.float4_e2m1fn_x4
+ALU = mybir.AluOpType
+ACT = mybir.ActivationFunctionType
+
+P = 128
+ITEMS = 1024
+FEATS = 1024
+OUTS = 1024
+K_PASS = 512
+GROUPS = FEATS // K_PASS
+ITEM_TILES = ITEMS // P
+N_MOVE = 512
+HALVES = ITEMS // N_MOVE
+TILES_PER_HALF = N_MOVE // P
+CHUNKS = OUTS // P
+BN_EPS = 1e-5
+SELF, NEIGH = 0, 1
+EARLY_CHUNKS = 3
+LAG = 2
+
+FLOPS = 2 * ITEMS * (2 * FEATS) * OUTS
+
+
+def tile_dogtaitujuanji_pb_kernel(
+    tc, h_sage, w1b_words, w1b_scales, w2b_words, w2b_scales, gamma, beta, out
+):
+    nc = tc.nc
+    words_in = {SELF: w2b_words, NEIGH: w1b_words}
+    scales_in = {SELF: w2b_scales, NEIGH: w1b_scales}
+
+    with ExitStack() as ctx:
+        ctx.enter_context(tc.manual_schedule())
+        keep = ctx.enter_context(tc.tile_pool(name="keep", bufs=1))
+        stage = ctx.enter_context(tc.tile_pool(name="stage", bufs=4))
+        small = ctx.enter_context(tc.tile_pool(name="small", bufs=4))
+        result = ctx.enter_context(tc.tile_pool(name="result", bufs=6))
+        psum_sums = ctx.enter_context(tc.psum_pool(name="psum_sums", bufs=6))
+        psum_flip = ctx.enter_context(tc.psum_pool(name="psum_flip", bufs=2))
+
+        w_planes = keep.tile([P, 2, GROUPS, OUTS], U8, align_bytes=64)
+        nc.vector.memset(w_planes[:].rearrange("p s g n -> p (s g n)").bitcast(I32), 0)
+        gb_rows = keep.tile([P, P], BF16)
+        nc.vector.memset(gb_rows[:], 0.0)
+        warm = keep.tile([P, 1], F32)
+        nc.vector.memset(warm[:], 0.0)
+
+        h_tiles = {}
+        w_words = {}
+
+        def load_scales(src):
+            by_row = scales_in[src].rearrange("g q n -> q g n")
+            for r in range(4):
+                nc.sync.dma_start(
+                    out=w_planes[r:P:32, src, :, :].bitcast(I32), in_=by_row[r:16:4, :, :].bitcast(I32)
+                )
+
+        def load_items(j):
+            h_tiles[j] = keep.tile([P, 3, FEATS], BF16, name="h%d" % j)
+            nc.sync.dma_start(out=h_tiles[j][:], in_=h_sage[j * P : (j + 1) * P, :, :])
+
+        def load_words(src):
+            w_words[src] = keep.tile([P, GROUPS, 2 * OUTS], U8, name="w%d" % src, align_bytes=64)
+            nc.sync.dma_start(
+                out=w_words[src][:].bitcast(I32), in_=words_in[src].rearrange("g p b -> p g b").bitcast(I32)
+            )
+
+        load_scales(SELF)
+        load_scales(NEIGH)
+        for j in range(TILES_PER_HALF):
+            load_items(j)
+        load_words(SELF)
+        load_words(NEIGH)
+        for j in range(TILES_PER_HALF, ITEM_TILES):
+            load_items(j)
+
+        ident_f32 = keep.tile([P, P], F32)
+        make_identity(nc, ident_f32[:])
+        ident_bf16 = keep.tile([P, P], BF16)
+        make_identity(nc, ident_bf16[:])
+        neg_half = keep.tile([P, 1], F32)
+        nc.gpsimd.memset(neg_half[:], -0.5)
+        nc.gpsimd.dma_start(out=gb_rows[0:CHUNKS, :], in_=gamma.rearrange("(c f) -> c f", f=P))
+        nc.gpsimd.dma_start(out=gb_rows[CHUNKS : 2 * CHUNKS, :], in_=beta.rearrange("(c f) -> c f", f=P))
+        nc.scalar.activation(out=warm[:], in_=warm[:], func=ACT.Sigmoid)
+
+        gamma_beta = keep.tile([P, 2 * CHUNKS], F32)
+        neg_gamma = keep.tile([P, CHUNKS], F32)
+
+        def spread_gamma_beta():
+            gb_bank = psum_flip.tile([P, P], BF16, tag="flip")
+            nc.tensor.transpose(gb_bank[:], gb_rows[:], ident_bf16[:])
+            nc.vector.tensor_copy(out=gamma_beta[:], in_=gb_bank[:, 0 : 2 * CHUNKS])
+            nc.vector.tensor_scalar(
+                out=neg_gamma[:], in0=gamma_beta[:, 0:CHUNKS], scalar1=-1.0, scalar2=None, op0=ALU.mult
+            )
+
+        x_codes = {}
+        x_planes = {}
+        for src in (SELF, NEIGH):
+            x_codes[src] = keep.tile([P, GROUPS, ITEMS], U32, name="x_codes%d" % src, align_bytes=64)
+            x_planes[src] = keep.tile([P, GROUPS, ITEMS], U8, name="x_planes%d" % src, align_bytes=64)
+        neigh_tiles = {}
+        grouped = {}
+
+        def average(j):
+            hop_sum = stage.tile([P, FEATS], BF16)
+            nc.vector.tensor_tensor(
+                out=hop_sum[:], in0=h_tiles[j][:, 1, :], in1=h_tiles[j][:, 2, :], op=ALU.add
+            )
+            neigh_tiles[j] = stage.tile([P, FEATS], BF16, name="neigh")
+            nc.vector.tensor_scalar(
+                out=neigh_tiles[j][:], in0=hop_sum[:], scalar1=0.5, scalar2=None, op0=ALU.mult
+            )
+
+        def flip(j):
+            by_item = {SELF: h_tiles[j][:, 0, :], NEIGH: neigh_tiles[j][:]}
+            for src in (SELF, NEIGH):
+                pairs = by_item[src].bitcast(F32)
+                bank = psum_flip.tile([P, GROUPS, 2, P], F32, tag="flip")
+                for g in range(GROUPS):
+                    for u in range(2):
+                        nc.tensor.transpose(
+                            bank[:, g, u, :], pairs[:, 256 * g + u : 256 * (g + 1) : 2], ident_f32[:]
+                        )
+                grouped[(j, src)] = stage.tile([P, GROUPS, P, 4], BF16, name="grouped%d" % src, align_bytes=64)
+                nc.scalar.copy(
+                    out=grouped[(j, src)][:]
+                    .rearrange("p g i t -> p (g i t)")
+                    .bitcast(F32)
+                    .rearrange("p (g i u) -> p g i u", g=GROUPS, u=2),
+                    in_=bank[:].rearrange("p g u i -> p g i u"),
+                )
+
+        def quantise(j):
+            for src in (SELF, NEIGH):
+                for g in range(GROUPS):
+                    nc.vector.quantize_mx(
+                        out=x_codes[src][:, g, j * P : (j + 1) * P].bitcast(FP8X4),
+                        scales=x_planes[src][:, g, j * P : (j + 1) * P],
+                        in_=grouped[(j, src)][:, g, :, :].rearrange("p i t -> p (i t)"),
+                    )
+
+        sums = {}
+        stats = {}
+        passes = [(src, g) for src in (SELF, NEIGH) for g in range(GROUPS)]
+
+        def multiply(c, half):
+            sums[(c, half)] = psum_sums.tile([P, N_MOVE], F32, tag="sums", name="sums")
+            for n, (src, g) in enumerate(passes):
+                nc.tensor.matmul_mx(
+                    out=sums[(c, half)][:],
+                    lhsT=w_words[src][:, g, 2 * P * c : 2 * P * (c + 1)].bitcast(FP4X4),
+                    lhsT_scale=w_planes[:, src, g, P * c : P * (c + 1)],
+                    rhs=x_codes[src][:, g, N_MOVE * half : N_MOVE * (half + 1)].bitcast(FP8X4),
+                    rhs_scale=x_planes[src][:, g, N_MOVE * half : N_MOVE * (half + 1)],
+                    start=(n == 0),
+                    stop=(n == len(passes) - 1),
+                )
+
+        def measure(c, half):
+            if half == 0:
+                stats[c] = small.tile([P, HALVES, 6], F32, name="stats")
+            nc.vector.bn_stats(out=stats[c][:, half, :], in_=sums[(c, half)][:])
+
+        mean_var = {}
+        rstd = {}
+        sigmoids = {}
+
+        def start_normalise(c):
+            mean_var[c] = small.tile([P, 2], F32, name="mean_var")
+            nc.vector.bn_aggr(out=mean_var[c][:], in_=stats[c][:].rearrange("p h s -> p (h s)"))
+            var_eps = small.tile([P, 1], F32)
+            nc.vector.tensor_scalar(
+                out=var_eps[:], in0=mean_var[c][:, 1:2], scalar1=BN_EPS, scalar2=None, op0=ALU.add
+            )
+            rstd[c] = small.tile([P, 1], F32, name="rstd")
+            nc.gpsimd.tensor_tensor(out=rstd[c][:], in0=var_eps[:], in1=neg_half[:], op=ALU.pow)
+
+        def finish_normalise(c):
+            affine = small.tile([P, 3], F32)
+            nc.vector.tensor_tensor(
+                out=affine[:, 0:1], in0=rstd[c][:], in1=gamma_beta[:, c : c + 1], op=ALU.mult
+            )
+            nc.vector.tensor_tensor(
+                out=affine[:, 1:2], in0=rstd[c][:], in1=neg_gamma[:, c : c + 1], op=ALU.mult
+            )
+            nc.vector.scalar_tensor_tensor(
+                out=affine[:, 2:3],
+                in0=mean_var[c][:, 0:1],
+                scalar=affine[:, 1:2],
+                in1=gamma_beta[:, CHUNKS + c : CHUNKS + c + 1],
+                op0=ALU.mult,
+                op1=ALU.add,
+            )
+            for half in range(HALVES):
+                sigmoids[(c, half)] = result.tile([P, N_MOVE], F32, name="sigmoid")
+                nc.scalar.activation(
+                    out=sigmoids[(c, half)][:],
+                    in_=sums[(c, half)][:],
+                    func=ACT.Sigmoid,
+                    bias=affine[:, 2:3],
+                    scale=affine[:, 0:1],
+                )
+
+        out_view = out.rearrange("(j p) f -> p j f", p=P)
+
+        def flip_back_and_store(c):
+            for half in range(HALVES):
+                bank = psum_flip.tile([P, TILES_PER_HALF, P], F32, tag="flip")
+                for i in range(TILES_PER_HALF):
+                    nc.tensor.transpose(bank[:, i, :], sigmoids[(c, half)][:, i * P : (i + 1) * P], ident_f32[:])
+                rows_out = result.tile([P, TILES_PER_HALF, P], F32)
+                if half == 0:
+                    nc.vector.tensor_copy(out=rows_out[:], in_=bank[:])
+                else:
+                    nc.scalar.copy(out=rows_out[:], in_=bank[:])
+                nc.sync.dma_start(
+                    out=out_view[:, TILES_PER_HALF * half : TILES_PER_HALF * (half + 1), c * P : (c + 1) * P],
+                    in_=rows_out[:],
+                )
+
+        for j in range(ITEM_TILES + 1):
+            if j < ITEM_TILES:
+                average(j)
+                flip(j)
+            if j == 2:
+                spread_gamma_beta()
+            if j >= 1:
+                quantise(j - 1)
+            if 0 <= j - TILES_PER_HALF - 1 < EARLY_CHUNKS:
+                measure(j - TILES_PER_HALF - 1, 0)
+            if 0 <= j - TILES_PER_HALF < EARLY_CHUNKS:
+                multiply(j - TILES_PER_HALF, 0)
+        for c in range(CHUNKS + LAG):
+            if c < CHUNKS:
+                if c >= EARLY_CHUNKS:
+                    multiply(c, 0)
+                    measure(c, 0)
+                multiply(c, 1)
+                measure(c, 1)
+                start_normalise(c)
+            if c >= LAG:
+                flip_back_and_store(c - LAG)
+            if c < CHUNKS:
+                finish_normalise(c)

@@ -26,7 +26,7 @@ TILES_PER_HALF = N_MOVE // P
 CHUNKS = OUTS // P
 BN_EPS = 1e-5
 SELF, NEIGH = 0, 1
-EARLY_CHUNKS = 3
+EARLY_CHUNKS = 4
 LAG = 2
 
 FLOPS = 2 * ITEMS * (2 * FEATS) * OUTS
@@ -45,15 +45,17 @@ def tile_dogtaitujuanji_pb_kernel(
         stage = ctx.enter_context(tc.tile_pool(name="stage", bufs=4))
         small = ctx.enter_context(tc.tile_pool(name="small", bufs=4))
         result = ctx.enter_context(tc.tile_pool(name="result", bufs=6))
-        psum_sums = ctx.enter_context(tc.psum_pool(name="psum_sums", bufs=6))
-        psum_flip = ctx.enter_context(tc.psum_pool(name="psum_flip", bufs=2))
+        psum = ctx.enter_context(tc.psum_pool(name="psum", bufs=8))
 
-        w_planes = keep.tile([P, 2, GROUPS, OUTS], U8, align_bytes=64)
-        nc.vector.memset(w_planes[:].rearrange("p s g n -> p (s g n)").bitcast(I32), 0)
         gb_rows = keep.tile([P, P], BF16)
         nc.vector.memset(gb_rows[:], 0.0)
+        w_planes = keep.tile([P, 2, GROUPS, OUTS], U8, align_bytes=64)
+        nc.vector.memset(w_planes[:].rearrange("p s g n -> p (s g n)").bitcast(I32), 0)
         warm = keep.tile([P, 1], F32)
         nc.vector.memset(warm[:], 0.0)
+
+        nc.scalar.dma_start(out=gb_rows[0:CHUNKS, :], in_=gamma.rearrange("(c f) -> c f", f=P))
+        nc.scalar.dma_start(out=gb_rows[CHUNKS : 2 * CHUNKS, :], in_=beta.rearrange("(c f) -> c f", f=P))
 
         h_tiles = {}
         w_words = {}
@@ -75,10 +77,12 @@ def tile_dogtaitujuanji_pb_kernel(
                 out=w_words[src][:].bitcast(I32), in_=words_in[src].rearrange("g p b -> p g b").bitcast(I32)
             )
 
+        load_items(0)
+        load_items(1)
         load_scales(SELF)
+        load_items(2)
+        load_items(3)
         load_scales(NEIGH)
-        for j in range(TILES_PER_HALF):
-            load_items(j)
         load_words(SELF)
         load_words(NEIGH)
         for j in range(TILES_PER_HALF, ITEM_TILES):
@@ -90,15 +94,13 @@ def tile_dogtaitujuanji_pb_kernel(
         make_identity(nc, ident_bf16[:])
         neg_half = keep.tile([P, 1], F32)
         nc.gpsimd.memset(neg_half[:], -0.5)
-        nc.gpsimd.dma_start(out=gb_rows[0:CHUNKS, :], in_=gamma.rearrange("(c f) -> c f", f=P))
-        nc.gpsimd.dma_start(out=gb_rows[CHUNKS : 2 * CHUNKS, :], in_=beta.rearrange("(c f) -> c f", f=P))
         nc.scalar.activation(out=warm[:], in_=warm[:], func=ACT.Sigmoid)
 
         gamma_beta = keep.tile([P, 2 * CHUNKS], F32)
         neg_gamma = keep.tile([P, CHUNKS], F32)
 
         def spread_gamma_beta():
-            gb_bank = psum_flip.tile([P, P], BF16, tag="flip")
+            gb_bank = psum.tile([P, P], BF16, tag="bank")
             nc.tensor.transpose(gb_bank[:], gb_rows[:], ident_bf16[:])
             nc.vector.tensor_copy(out=gamma_beta[:], in_=gb_bank[:, 0 : 2 * CHUNKS])
             nc.vector.tensor_scalar(
@@ -127,7 +129,7 @@ def tile_dogtaitujuanji_pb_kernel(
             by_item = {SELF: h_tiles[j][:, 0, :], NEIGH: neigh_tiles[j][:]}
             for src in (SELF, NEIGH):
                 pairs = by_item[src].bitcast(F32)
-                bank = psum_flip.tile([P, GROUPS, 2, P], F32, tag="flip")
+                bank = psum.tile([P, GROUPS, 2, P], F32, tag="bank")
                 for g in range(GROUPS):
                     for u in range(2):
                         nc.tensor.transpose(
@@ -156,7 +158,7 @@ def tile_dogtaitujuanji_pb_kernel(
         passes = [(src, g) for src in (SELF, NEIGH) for g in range(GROUPS)]
 
         def multiply(c, half):
-            sums[(c, half)] = psum_sums.tile([P, N_MOVE], F32, tag="sums", name="sums")
+            sums[(c, half)] = psum.tile([P, N_MOVE], F32, tag="bank", name="sums")
             for n, (src, g) in enumerate(passes):
                 nc.tensor.matmul_mx(
                     out=sums[(c, half)][:],
@@ -217,7 +219,7 @@ def tile_dogtaitujuanji_pb_kernel(
 
         def flip_back_and_store(c):
             for half in range(HALVES):
-                bank = psum_flip.tile([P, TILES_PER_HALF, P], F32, tag="flip")
+                bank = psum.tile([P, TILES_PER_HALF, P], F32, tag="bank")
                 for i in range(TILES_PER_HALF):
                     nc.tensor.transpose(bank[:, i, :], sigmoids[(c, half)][:, i * P : (i + 1) * P], ident_f32[:])
                 rows_out = result.tile([P, TILES_PER_HALF, P], F32)
@@ -234,7 +236,7 @@ def tile_dogtaitujuanji_pb_kernel(
             if j < ITEM_TILES:
                 average(j)
                 flip(j)
-            if j == 2:
+            if j == 5:
                 spread_gamma_beta()
             if j >= 1:
                 quantise(j - 1)

@@ -26,7 +26,9 @@ TILES_PER_HALF = N_MOVE // P
 CHUNKS = OUTS // P
 BN_EPS = 1e-5
 SELF, NEIGH = 0, 1
-EARLY_CHUNKS = 4
+EARLY_CHUNKS = 5
+W_PARTS = 2
+CHUNKS_PER_PART = CHUNKS // W_PARTS
 LAG = 2
 
 FLOPS = 2 * ITEMS * (2 * FEATS) * OUTS
@@ -71,10 +73,12 @@ def tile_dogtaitujuanji_pb_kernel(
             h_tiles[j] = keep.tile([P, 3, FEATS], BF16, name="h%d" % j)
             nc.sync.dma_start(out=h_tiles[j][:], in_=h_sage[j * P : (j + 1) * P, :, :])
 
-        def load_words(src):
-            w_words[src] = keep.tile([P, GROUPS, 2 * OUTS], U8, name="w%d" % src, align_bytes=64)
+        def load_words(src, part):
+            width = 2 * P * CHUNKS_PER_PART
+            w_words[(src, part)] = keep.tile([P, GROUPS, width], U8, name="w%d_%d" % (src, part), align_bytes=64)
             nc.sync.dma_start(
-                out=w_words[src][:].bitcast(I32), in_=words_in[src].rearrange("g p b -> p g b").bitcast(I32)
+                out=w_words[(src, part)][:].bitcast(I32),
+                in_=words_in[src].rearrange("g p b -> p g b")[:, :, part * width : (part + 1) * width].bitcast(I32),
             )
 
         load_items(0)
@@ -83,10 +87,12 @@ def tile_dogtaitujuanji_pb_kernel(
         load_items(2)
         load_items(3)
         load_scales(NEIGH)
-        load_words(SELF)
-        load_words(NEIGH)
+        load_words(SELF, 0)
+        load_words(NEIGH, 0)
         for j in range(TILES_PER_HALF, ITEM_TILES):
             load_items(j)
+        load_words(SELF, 1)
+        load_words(NEIGH, 1)
 
         ident_f32 = keep.tile([P, P], F32)
         make_identity(nc, ident_f32[:])
@@ -154,7 +160,7 @@ def tile_dogtaitujuanji_pb_kernel(
                     )
 
         sums = {}
-        stats = {}
+        stats = keep.tile([P, CHUNKS, HALVES, 6], F32)
         passes = [(src, g) for src in (SELF, NEIGH) for g in range(GROUPS)]
 
         def multiply(c, half):
@@ -162,7 +168,9 @@ def tile_dogtaitujuanji_pb_kernel(
             for n, (src, g) in enumerate(passes):
                 nc.tensor.matmul_mx(
                     out=sums[(c, half)][:],
-                    lhsT=w_words[src][:, g, 2 * P * c : 2 * P * (c + 1)].bitcast(FP4X4),
+                    lhsT=w_words[(src, c // CHUNKS_PER_PART)][
+                        :, g, 2 * P * (c % CHUNKS_PER_PART) : 2 * P * (c % CHUNKS_PER_PART + 1)
+                    ].bitcast(FP4X4),
                     lhsT_scale=w_planes[:, src, g, P * c : P * (c + 1)],
                     rhs=x_codes[src][:, g, N_MOVE * half : N_MOVE * (half + 1)].bitcast(FP8X4),
                     rhs_scale=x_planes[src][:, g, N_MOVE * half : N_MOVE * (half + 1)],
@@ -171,9 +179,7 @@ def tile_dogtaitujuanji_pb_kernel(
                 )
 
         def measure(c, half):
-            if half == 0:
-                stats[c] = small.tile([P, HALVES, 6], F32, name="stats")
-            nc.vector.bn_stats(out=stats[c][:, half, :], in_=sums[(c, half)][:])
+            nc.vector.bn_stats(out=stats[:, c, half, :], in_=sums[(c, half)][:])
 
         mean_var = {}
         rstd = {}
@@ -181,7 +187,7 @@ def tile_dogtaitujuanji_pb_kernel(
 
         def start_normalise(c):
             mean_var[c] = small.tile([P, 2], F32, name="mean_var")
-            nc.vector.bn_aggr(out=mean_var[c][:], in_=stats[c][:].rearrange("p h s -> p (h s)"))
+            nc.vector.bn_aggr(out=mean_var[c][:], in_=stats[:, c, :, :].rearrange("p h s -> p (h s)"))
             var_eps = small.tile([P, 1], F32)
             nc.vector.tensor_scalar(
                 out=var_eps[:], in0=mean_var[c][:, 1:2], scalar1=BN_EPS, scalar2=None, op0=ALU.add
@@ -232,18 +238,27 @@ def tile_dogtaitujuanji_pb_kernel(
                     in_=rows_out[:],
                 )
 
-        for j in range(ITEM_TILES + 1):
-            if j < ITEM_TILES:
-                average(j)
-                flip(j)
-            if j == 5:
+        for j in range(TILES_PER_HALF):
+            average(j)
+            flip(j)
+            if j == 1:
                 spread_gamma_beta()
             if j >= 1:
                 quantise(j - 1)
-            if 0 <= j - TILES_PER_HALF - 1 < EARLY_CHUNKS:
-                measure(j - TILES_PER_HALF - 1, 0)
-            if 0 <= j - TILES_PER_HALF < EARLY_CHUNKS:
-                multiply(j - TILES_PER_HALF, 0)
+        quantise(TILES_PER_HALF - 1)
+        for i in range(TILES_PER_HALF):
+            j = TILES_PER_HALF + i
+            multiply(i, 0)
+            average(j)
+            flip(j)
+            if i >= 1:
+                quantise(j - 1)
+            measure(i, 0)
+        for c in range(TILES_PER_HALF, EARLY_CHUNKS):
+            multiply(c, 0)
+        quantise(ITEM_TILES - 1)
+        for c in range(TILES_PER_HALF, EARLY_CHUNKS):
+            measure(c, 0)
         for c in range(CHUNKS + LAG):
             if c < CHUNKS:
                 if c >= EARLY_CHUNKS:

@@ -102,15 +102,18 @@ def tile_dogtaitujuanji_pb_kernel(
         nc.gpsimd.memset(neg_half[:], -0.5)
         nc.scalar.activation(out=warm[:], in_=warm[:], func=ACT.Sigmoid)
 
-        gamma_beta = keep.tile([P, 2 * CHUNKS], F32)
+        factors = keep.tile([P, CHUNKS, 2], F32)
+        addends = keep.tile([P, CHUNKS, 2], F32)
+        nc.vector.memset(addends[:], 0.0)
         neg_gamma = keep.tile([P, CHUNKS], F32)
 
         def spread_gamma_beta():
             gb_bank = psum.tile([P, P], BF16, tag="bank")
             nc.tensor.transpose(gb_bank[:], gb_rows[:], ident_bf16[:])
-            nc.vector.tensor_copy(out=gamma_beta[:], in_=gb_bank[:, 0 : 2 * CHUNKS])
+            nc.vector.tensor_copy(out=factors[:, :, 0], in_=gb_bank[:, 0:CHUNKS])
+            nc.vector.tensor_copy(out=addends[:, :, 1], in_=gb_bank[:, CHUNKS : 2 * CHUNKS])
             nc.vector.tensor_scalar(
-                out=neg_gamma[:], in0=gamma_beta[:, 0:CHUNKS], scalar1=-1.0, scalar2=None, op0=ALU.mult
+                out=neg_gamma[:], in0=gb_bank[:, 0:CHUNKS], scalar1=-1.0, scalar2=None, op0=ALU.mult
             )
 
         x_codes = {}
@@ -194,20 +197,17 @@ def tile_dogtaitujuanji_pb_kernel(
             )
             rstd[c] = small.tile([P, 1], F32, name="rstd")
             nc.gpsimd.tensor_tensor(out=rstd[c][:], in0=var_eps[:], in1=neg_half[:], op=ALU.pow)
+            nc.vector.tensor_tensor(
+                out=factors[:, c, 1:2], in0=mean_var[c][:, 0:1], in1=neg_gamma[:, c : c + 1], op=ALU.mult
+            )
 
         def finish_normalise(c):
-            affine = small.tile([P, 3], F32)
-            nc.vector.tensor_tensor(
-                out=affine[:, 0:1], in0=rstd[c][:], in1=gamma_beta[:, c : c + 1], op=ALU.mult
-            )
-            nc.vector.tensor_tensor(
-                out=affine[:, 1:2], in0=rstd[c][:], in1=neg_gamma[:, c : c + 1], op=ALU.mult
-            )
+            affine = small.tile([P, 2], F32)
             nc.vector.scalar_tensor_tensor(
-                out=affine[:, 2:3],
-                in0=mean_var[c][:, 0:1],
-                scalar=affine[:, 1:2],
-                in1=gamma_beta[:, CHUNKS + c : CHUNKS + c + 1],
+                out=affine[:],
+                in0=factors[:, c, :],
+                scalar=rstd[c][:],
+                in1=addends[:, c, :],
                 op0=ALU.mult,
                 op1=ALU.add,
             )
@@ -217,7 +217,7 @@ def tile_dogtaitujuanji_pb_kernel(
                     out=sigmoids[(c, half)][:],
                     in_=sums[(c, half)][:],
                     func=ACT.Sigmoid,
-                    bias=affine[:, 2:3],
+                    bias=affine[:, 1:2],
                     scale=affine[:, 0:1],
                 )
 

@@ -29,7 +29,7 @@ SELF, NEIGH = 0, 1
 EARLY_CHUNKS = 5
 W_PARTS = 2
 CHUNKS_PER_PART = CHUNKS // W_PARTS
-LAG = 2
+LAG = 3
 
 FLOPS = 2 * ITEMS * (2 * FEATS) * OUTS
 
@@ -46,7 +46,7 @@ def tile_dogtaitujuanji_pb_kernel(
         keep = ctx.enter_context(tc.tile_pool(name="keep", bufs=1))
         stage = ctx.enter_context(tc.tile_pool(name="stage", bufs=4))
         small = ctx.enter_context(tc.tile_pool(name="small", bufs=4))
-        result = ctx.enter_context(tc.tile_pool(name="result", bufs=6))
+        result = ctx.enter_context(tc.tile_pool(name="result", bufs=8))
         psum = ctx.enter_context(tc.psum_pool(name="psum", bufs=8))
 
         gb_rows = keep.tile([P, P], BF16)
@@ -188,9 +188,16 @@ def tile_dogtaitujuanji_pb_kernel(
         rstd = {}
         sigmoids = {}
 
-        def start_normalise(c):
+        def park(c):
+            parked = keep.tile([P, N_MOVE], F32, name="parked%d" % c)
+            nc.scalar.copy(out=parked[:], in_=sums[(c, 0)][:])
+            sums[(c, 0)] = parked
+
+        def aggregate(c):
             mean_var[c] = small.tile([P, 2], F32, name="mean_var")
             nc.vector.bn_aggr(out=mean_var[c][:], in_=stats[:, c, :, :].rearrange("p h s -> p (h s)"))
+
+        def take_power(c):
             var_eps = small.tile([P, 1], F32)
             nc.vector.tensor_scalar(
                 out=var_eps[:], in0=mean_var[c][:, 1:2], scalar1=BN_EPS, scalar2=None, op0=ALU.add
@@ -259,6 +266,8 @@ def tile_dogtaitujuanji_pb_kernel(
         quantise(ITEM_TILES - 1)
         for c in range(TILES_PER_HALF, EARLY_CHUNKS):
             measure(c, 0)
+        for c in range(TILES_PER_HALF, EARLY_CHUNKS):
+            park(c)
         for c in range(CHUNKS + LAG):
             if c < CHUNKS:
                 if c >= EARLY_CHUNKS:
@@ -266,8 +275,13 @@ def tile_dogtaitujuanji_pb_kernel(
                     measure(c, 0)
                 multiply(c, 1)
                 measure(c, 1)
-                start_normalise(c)
-            if c >= LAG:
-                flip_back_and_store(c - LAG)
+            if 1 <= c <= CHUNKS:
+                finish_normalise(c - 1)
             if c < CHUNKS:
-                finish_normalise(c)
+                aggregate(c)
+            if c == CHUNKS - 1:
+                take_power(c)
+            if 0 <= c - LAG < CHUNKS:
+                flip_back_and_store(c - LAG)
+            if c < CHUNKS - 1:
+                take_power(c)

@@ -29,7 +29,8 @@ SELF, NEIGH = 0, 1
 EARLY_CHUNKS = 5
 W_PARTS = 2
 CHUNKS_PER_PART = CHUNKS // W_PARTS
-LAG = 3
+LAG_SHORT_STEPS = 3
+LAG_LONG_STEPS = 2
 
 FLOPS = 2 * ITEMS * (2 * FEATS) * OUTS
 
@@ -131,7 +132,11 @@ def tile_dogtaitujuanji_pb_kernel(
             )
             neigh_tiles[j] = stage.tile([P, FEATS], BF16, name="neigh")
             nc.vector.tensor_scalar(
-                out=neigh_tiles[j][:], in0=hop_sum[:], scalar1=0.5, scalar2=None, op0=ALU.mult
+                out=neigh_tiles[j][:].rearrange("p (u w e) -> p u w e", u=2, e=2),
+                in0=hop_sum[:].rearrange("p (w u e) -> p u w e", u=2, e=2),
+                scalar1=0.5,
+                scalar2=None,
+                op0=ALU.mult,
             )
 
         def flip(j):
@@ -141,9 +146,11 @@ def tile_dogtaitujuanji_pb_kernel(
                 bank = psum.tile([P, GROUPS, 2, P], F32, tag="bank")
                 for g in range(GROUPS):
                     for u in range(2):
-                        nc.tensor.transpose(
-                            bank[:, g, u, :], pairs[:, 256 * g + u : 256 * (g + 1) : 2], ident_f32[:]
-                        )
+                        if src == SELF:
+                            words = pairs[:, 256 * g + u : 256 * (g + 1) : 2]
+                        else:
+                            words = pairs[:, 256 * u + P * g : 256 * u + P * (g + 1)]
+                        nc.tensor.transpose(bank[:, g, u, :], words, ident_f32[:])
                 grouped[(j, src)] = stage.tile([P, GROUPS, P, 4], BF16, name="grouped%d" % src, align_bytes=64)
                 nc.scalar.copy(
                     out=grouped[(j, src)][:]
@@ -268,20 +275,24 @@ def tile_dogtaitujuanji_pb_kernel(
             measure(c, 0)
         for c in range(TILES_PER_HALF, EARLY_CHUNKS):
             park(c)
-        for c in range(CHUNKS + LAG):
+        def last_back(c):
+            return c - (LAG_SHORT_STEPS if c < EARLY_CHUNKS else LAG_LONG_STEPS)
+
+        for c in range(CHUNKS + LAG_LONG_STEPS):
+            if EARLY_CHUNKS <= c < CHUNKS:
+                multiply(c, 0)
+                measure(c, 0)
+                finish_normalise(c - 1)
             if c < CHUNKS:
-                if c >= EARLY_CHUNKS:
-                    multiply(c, 0)
-                    measure(c, 0)
                 multiply(c, 1)
                 measure(c, 1)
-            if 1 <= c <= CHUNKS:
+            if 1 <= c < EARLY_CHUNKS or c == CHUNKS:
                 finish_normalise(c - 1)
             if c < CHUNKS:
                 aggregate(c)
             if c == CHUNKS - 1:
                 take_power(c)
-            if 0 <= c - LAG < CHUNKS:
-                flip_back_and_store(c - LAG)
+            for b in range(max(0, last_back(c - 1) + 1), min(CHUNKS - 1, last_back(c)) + 1):
+                flip_back_and_store(b)
             if c < CHUNKS - 1:
                 take_power(c)

@@ -125,15 +125,19 @@ def tile_dogtaitujuanji_pb_kernel(
         neigh_tiles = {}
         grouped = {}
 
-        def average(j):
-            hop_sum = stage.tile([P, FEATS], BF16)
+        hop_sums = {}
+
+        def add_hops(j):
+            hop_sums[j] = stage.tile([P, FEATS], BF16, name="hop_sum")
             nc.vector.tensor_tensor(
-                out=hop_sum[:], in0=h_tiles[j][:, 1, :], in1=h_tiles[j][:, 2, :], op=ALU.add
+                out=hop_sums[j][:], in0=h_tiles[j][:, 1, :], in1=h_tiles[j][:, 2, :], op=ALU.add
             )
+
+        def halve(j):
             neigh_tiles[j] = stage.tile([P, FEATS], BF16, name="neigh")
             nc.vector.tensor_scalar(
                 out=neigh_tiles[j][:].rearrange("p (u w e) -> p u w e", u=2, e=2),
-                in0=hop_sum[:].rearrange("p (w u e) -> p u w e", u=2, e=2),
+                in0=hop_sums[j][:].rearrange("p (w u e) -> p u w e", u=2, e=2),
                 scalar1=0.5,
                 scalar2=None,
                 op0=ALU.mult,
@@ -160,14 +164,13 @@ def tile_dogtaitujuanji_pb_kernel(
                     in_=bank[:].rearrange("p g u i -> p g i u"),
                 )
 
-        def quantise(j):
-            for src in (SELF, NEIGH):
-                for g in range(GROUPS):
-                    nc.vector.quantize_mx(
-                        out=x_codes[src][:, g, j * P : (j + 1) * P].bitcast(FP8X4),
-                        scales=x_planes[src][:, g, j * P : (j + 1) * P],
-                        in_=grouped[(j, src)][:, g, :, :].rearrange("p i t -> p (i t)"),
-                    )
+        def quantise(j, src):
+            for g in range(GROUPS):
+                nc.vector.quantize_mx(
+                    out=x_codes[src][:, g, j * P : (j + 1) * P].bitcast(FP8X4),
+                    scales=x_planes[src][:, g, j * P : (j + 1) * P],
+                    in_=grouped[(j, src)][:, g, :, :].rearrange("p i t -> p (i t)"),
+                )
 
         sums = {}
         stats = keep.tile([P, CHUNKS, HALVES, 6], F32)
@@ -253,24 +256,32 @@ def tile_dogtaitujuanji_pb_kernel(
                 )
 
         for j in range(TILES_PER_HALF):
-            average(j)
+            add_hops(j)
+            if j >= 1:
+                quantise(j - 1, SELF)
+            halve(j)
             flip(j)
             if j == 1:
                 spread_gamma_beta()
             if j >= 1:
-                quantise(j - 1)
-        quantise(TILES_PER_HALF - 1)
+                quantise(j - 1, NEIGH)
+        quantise(TILES_PER_HALF - 1, SELF)
+        quantise(TILES_PER_HALF - 1, NEIGH)
         for i in range(TILES_PER_HALF):
             j = TILES_PER_HALF + i
             multiply(i, 0)
-            average(j)
+            add_hops(j)
+            if i >= 1:
+                quantise(j - 1, SELF)
+            halve(j)
             flip(j)
             if i >= 1:
-                quantise(j - 1)
+                quantise(j - 1, NEIGH)
             measure(i, 0)
         for c in range(TILES_PER_HALF, EARLY_CHUNKS):
             multiply(c, 0)
-        quantise(ITEM_TILES - 1)
+        quantise(ITEM_TILES - 1, SELF)
+        quantise(ITEM_TILES - 1, NEIGH)
         for c in range(TILES_PER_HALF, EARLY_CHUNKS):
             measure(c, 0)
         for c in range(TILES_PER_HALF, EARLY_CHUNKS):

@@ -218,6 +218,9 @@ def tile_dogtaitujuanji_pb_kernel(
                 out=factors[:, c, 1:2], in0=mean_var[c][:, 0:1], in1=neg_gamma[:, c : c + 1], op=ALU.mult
             )
 
+        def pieces_of(c):
+            return 2 * HALVES if c == CHUNKS - 1 else HALVES
+
         def finish_normalise(c):
             affine = small.tile([P, 2], F32)
             nc.vector.scalar_tensor_tensor(
@@ -230,9 +233,12 @@ def tile_dogtaitujuanji_pb_kernel(
             )
             for half in range(HALVES):
                 sigmoids[(c, half)] = result.tile([P, N_MOVE], F32, name="sigmoid")
+            width = ITEMS // pieces_of(c)
+            for piece in range(pieces_of(c)):
+                half, low = divmod(piece * width, N_MOVE)
                 nc.scalar.activation(
-                    out=sigmoids[(c, half)][:],
-                    in_=sums[(c, half)][:],
+                    out=sigmoids[(c, half)][:, low : low + width],
+                    in_=sums[(c, half)][:, low : low + width],
                     func=ACT.Sigmoid,
                     bias=affine[:, 1:2],
                     scale=affine[:, 0:1],
@@ -241,18 +247,19 @@ def tile_dogtaitujuanji_pb_kernel(
         out_view = out.rearrange("(j p) f -> p j f", p=P)
 
         def flip_back_and_store(c):
-            for half in range(HALVES):
-                bank = psum.tile([P, TILES_PER_HALF, P], F32, tag="bank")
-                for i in range(TILES_PER_HALF):
-                    nc.tensor.transpose(bank[:, i, :], sigmoids[(c, half)][:, i * P : (i + 1) * P], ident_f32[:])
-                rows_out = result.tile([P, TILES_PER_HALF, P], F32)
-                if half == 0:
+            tiles = ITEM_TILES // pieces_of(c)
+            for piece in range(pieces_of(c)):
+                bank = psum.tile([P, tiles, P], F32, tag="bank")
+                for i in range(tiles):
+                    half, t = divmod(piece * tiles + i, TILES_PER_HALF)
+                    nc.tensor.transpose(bank[:, i, :], sigmoids[(c, half)][:, t * P : (t + 1) * P], ident_f32[:])
+                rows_out = result.tile([P, tiles, P], F32)
+                if piece < pieces_of(c) - 1:
                     nc.vector.tensor_copy(out=rows_out[:], in_=bank[:])
                 else:
                     nc.scalar.copy(out=rows_out[:], in_=bank[:])
                 nc.sync.dma_start(
-                    out=out_view[:, TILES_PER_HALF * half : TILES_PER_HALF * (half + 1), c * P : (c + 1) * P],
-                    in_=rows_out[:],
+                    out=out_view[:, tiles * piece : tiles * (piece + 1), c * P : (c + 1) * P], in_=rows_out[:]
                 )
 
         for j in range(TILES_PER_HALF):

@@ -143,14 +143,23 @@ def tile_dogtaitujuanji_pb_kernel(
                 op0=ALU.mult,
             )
 
+        self_ordered = {}
+
+        def order_self(j):
+            self_ordered[j] = stage.tile([P, FEATS], BF16, name="self_ordered")
+            nc.vector.tensor_copy(
+                out=self_ordered[j][:].bitcast(F32).rearrange("p (u w) -> p u w", u=2),
+                in_=h_tiles[j][:, 0, :].bitcast(F32).rearrange("p (w u) -> p u w", u=2),
+            )
+
         def flip(j):
-            by_item = {SELF: h_tiles[j][:, 0, :], NEIGH: neigh_tiles[j][:]}
+            by_item = {SELF: self_ordered[j][:] if j in self_ordered else h_tiles[j][:, 0, :], NEIGH: neigh_tiles[j][:]}
             for src in (SELF, NEIGH):
                 pairs = by_item[src].bitcast(F32)
                 bank = psum.tile([P, GROUPS, 2, P], F32, tag="bank")
                 for g in range(GROUPS):
                     for u in range(2):
-                        if src == SELF:
+                        if src == SELF and j not in self_ordered:
                             words = pairs[:, 256 * g + u : 256 * (g + 1) : 2]
                         else:
                             words = pairs[:, 256 * u + P * g : 256 * u + P * (g + 1)]
@@ -278,11 +287,11 @@ def tile_dogtaitujuanji_pb_kernel(
             j = TILES_PER_HALF + i
             multiply(i, 0)
             add_hops(j)
-            if i >= 1:
-                quantise(j - 1, SELF)
+            order_self(j)
             halve(j)
             flip(j)
             if i >= 1:
+                quantise(j - 1, SELF)
                 quantise(j - 1, NEIGH)
             measure(i, 0)
         for c in range(TILES_PER_HALF, EARLY_CHUNKS):

@@ -26,11 +26,27 @@ TILES_PER_HALF = N_MOVE // P
 CHUNKS = OUTS // P
 BN_EPS = 1e-5
 SELF, NEIGH = 0, 1
+STREAMED = 0
+PARKED = (4,)
+W1_BEFORE_TILE = 8
 EARLY_CHUNKS = 5
 W_PARTS = 2
 CHUNKS_PER_PART = CHUNKS // W_PARTS
 LAG_SHORT_STEPS = 3
 LAG_LONG_STEPS = 2
+HALVE_ON_SCALAR = False
+ORDER_SELF_TILES = (4, 5, 6, 7)
+SEAM_FILL = False
+EPS_IN_STATS = True
+AGGR_FIRST = True
+QUAD = 32
+VIA_BLOCKS = ()
+QUEUES = "sync"
+EARLY_STEPS = (0, 1, 2, 3)
+DEFER_STATS = False
+WEAVE_AHEAD = 1
+STORE_GROUPS = ((0,), (1,), (2,), (3,), (4,), (5,), (6,), (7,))
+GB_SPREAD_AT = 1
 
 FLOPS = 2 * ITEMS * (2 * FEATS) * OUTS
 
@@ -48,6 +64,8 @@ def tile_dogtaitujuanji_pb_kernel(
         stage = ctx.enter_context(tc.tile_pool(name="stage", bufs=4))
         small = ctx.enter_context(tc.tile_pool(name="small", bufs=4))
         result = ctx.enter_context(tc.tile_pool(name="result", bufs=8))
+        blocks = ctx.enter_context(tc.tile_pool(name="blocks", bufs=2))
+        wide = ctx.enter_context(tc.tile_pool(name="wide", bufs=4))
         psum = ctx.enter_context(tc.psum_pool(name="psum", bufs=8))
 
         gb_rows = keep.tile([P, P], BF16)
@@ -90,10 +108,12 @@ def tile_dogtaitujuanji_pb_kernel(
         load_scales(NEIGH)
         load_words(SELF, 0)
         load_words(NEIGH, 0)
-        for j in range(TILES_PER_HALF, ITEM_TILES):
-            load_items(j)
-        load_words(SELF, 1)
-        load_words(NEIGH, 1)
+        for j in range(TILES_PER_HALF, ITEM_TILES + 1):
+            if j == W1_BEFORE_TILE:
+                load_words(SELF, 1)
+                load_words(NEIGH, 1)
+            if j < ITEM_TILES:
+                load_items(j)
 
         ident_f32 = keep.tile([P, P], F32)
         make_identity(nc, ident_f32[:])
@@ -108,9 +128,14 @@ def tile_dogtaitujuanji_pb_kernel(
         nc.vector.memset(addends[:], 0.0)
         neg_gamma = keep.tile([P, CHUNKS], F32)
 
+        gb_banks = []
+
+        def flip_gamma_beta():
+            gb_banks.append(psum.tile([P, P], BF16, tag="bank", name="gb_bank"))
+            nc.tensor.transpose(gb_banks[0][:], gb_rows[:], ident_bf16[:])
+
         def spread_gamma_beta():
-            gb_bank = psum.tile([P, P], BF16, tag="bank")
-            nc.tensor.transpose(gb_bank[:], gb_rows[:], ident_bf16[:])
+            gb_bank = gb_banks[0]
             nc.vector.tensor_copy(out=factors[:, :, 0], in_=gb_bank[:, 0:CHUNKS])
             nc.vector.tensor_copy(out=addends[:, :, 1], in_=gb_bank[:, CHUNKS : 2 * CHUNKS])
             nc.vector.tensor_scalar(
@@ -128,12 +153,23 @@ def tile_dogtaitujuanji_pb_kernel(
         hop_sums = {}
 
         def add_hops(j):
+            if HALVE_ON_SCALAR:
+                neigh_tiles[j] = stage.tile([P, FEATS], BF16, name="neigh")
+                nc.vector.tensor_tensor(
+                    out=neigh_tiles[j][:].rearrange("p (u w e) -> p u w e", u=2, e=2),
+                    in0=h_tiles[j][:, 1, :].rearrange("p (w u e) -> p u w e", u=2, e=2),
+                    in1=h_tiles[j][:, 2, :].rearrange("p (w u e) -> p u w e", u=2, e=2),
+                    op=ALU.add,
+                )
+                return
             hop_sums[j] = stage.tile([P, FEATS], BF16, name="hop_sum")
             nc.vector.tensor_tensor(
                 out=hop_sums[j][:], in0=h_tiles[j][:, 1, :], in1=h_tiles[j][:, 2, :], op=ALU.add
             )
 
         def halve(j):
+            if HALVE_ON_SCALAR:
+                return
             neigh_tiles[j] = stage.tile([P, FEATS], BF16, name="neigh")
             nc.vector.tensor_scalar(
                 out=neigh_tiles[j][:].rearrange("p (u w e) -> p u w e", u=2, e=2),
@@ -165,6 +201,18 @@ def tile_dogtaitujuanji_pb_kernel(
                             words = pairs[:, 256 * u + P * g : 256 * u + P * (g + 1)]
                         nc.tensor.transpose(bank[:, g, u, :], words, ident_f32[:])
                 grouped[(j, src)] = stage.tile([P, GROUPS, P, 4], BF16, name="grouped%d" % src, align_bytes=64)
+                if src == NEIGH and HALVE_ON_SCALAR:
+                    for g in range(GROUPS):
+                        nc.scalar.activation(
+                            out=grouped[(j, src)][:, g, :, :].rearrange("p i (u e) -> p i u e", e=2),
+                            in_=bank[:, g, :, :]
+                            .rearrange("p u i -> p (u i)")
+                            .bitcast(BF16)
+                            .rearrange("p (u i e) -> p i u e", u=2, e=2),
+                            func=ACT.Copy,
+                            scale=0.5,
+                        )
+                    continue
                 nc.scalar.copy(
                     out=grouped[(j, src)][:]
                     .rearrange("p g i t -> p (g i t)")
@@ -200,6 +248,22 @@ def tile_dogtaitujuanji_pb_kernel(
                     stop=(n == len(passes) - 1),
                 )
 
+        def multiply_tile(c, j):
+            if j == 0:
+                sums[(c, 0)] = psum.tile([P, N_MOVE], F32, tag="bank", name="sums")
+            for n, (src, g) in enumerate(passes):
+                nc.tensor.matmul_mx(
+                    out=sums[(c, 0)][:, j * P : (j + 1) * P],
+                    lhsT=w_words[(src, c // CHUNKS_PER_PART)][
+                        :, g, 2 * P * (c % CHUNKS_PER_PART) : 2 * P * (c % CHUNKS_PER_PART + 1)
+                    ].bitcast(FP4X4),
+                    lhsT_scale=w_planes[:, src, g, P * c : P * (c + 1)],
+                    rhs=x_codes[src][:, g, j * P : (j + 1) * P].bitcast(FP8X4),
+                    rhs_scale=x_planes[src][:, g, j * P : (j + 1) * P],
+                    start=(n == 0),
+                    stop=(n == len(passes) - 1),
+                )
+
         def measure(c, half):
             nc.vector.bn_stats(out=stats[:, c, half, :], in_=sums[(c, half)][:])
 
@@ -216,7 +280,28 @@ def tile_dogtaitujuanji_pb_kernel(
             mean_var[c] = small.tile([P, 2], F32, name="mean_var")
             nc.vector.bn_aggr(out=mean_var[c][:], in_=stats[:, c, :, :].rearrange("p h s -> p (h s)"))
 
+        def lift(first, last):
+            nc.vector.tensor_scalar(
+                out=stats[:, first:last, 0, 2:3],
+                in0=stats[:, first:last, 0, 2:3],
+                scalar1=ITEMS * BN_EPS,
+                scalar2=None,
+                op0=ALU.add,
+            )
+
+        def power(c):
+            rstd[c] = small.tile([P, 1], F32, name="rstd")
+            nc.gpsimd.tensor_tensor(out=rstd[c][:], in0=mean_var[c][:, 1:2], in1=neg_half[:], op=ALU.pow)
+
+        def scale_mean(c):
+            nc.vector.tensor_tensor(
+                out=factors[:, c, 1:2], in0=mean_var[c][:, 0:1], in1=neg_gamma[:, c : c + 1], op=ALU.mult
+            )
+
         def take_power(c):
+            if EPS_IN_STATS:
+                scale_mean(c)
+                return
             var_eps = small.tile([P, 1], F32)
             nc.vector.tensor_scalar(
                 out=var_eps[:], in0=mean_var[c][:, 1:2], scalar1=BN_EPS, scalar2=None, op0=ALU.add
@@ -241,7 +326,7 @@ def tile_dogtaitujuanji_pb_kernel(
                 op1=ALU.add,
             )
             for half in range(HALVES):
-                sigmoids[(c, half)] = result.tile([P, N_MOVE], F32, name="sigmoid")
+                sigmoids[(c, half)] = result.tile([P, N_MOVE], F32, name="sigmoid", align_bytes=64)
             width = ITEMS // pieces_of(c)
             for piece in range(pieces_of(c)):
                 half, low = divmod(piece * width, N_MOVE)
@@ -255,6 +340,8 @@ def tile_dogtaitujuanji_pb_kernel(
 
         out_view = out.rearrange("(j p) f -> p j f", p=P)
 
+        rows_out = {}
+
         def flip_back_and_store(c):
             tiles = ITEM_TILES // pieces_of(c)
             for piece in range(pieces_of(c)):
@@ -262,46 +349,102 @@ def tile_dogtaitujuanji_pb_kernel(
                 for i in range(tiles):
                     half, t = divmod(piece * tiles + i, TILES_PER_HALF)
                     nc.tensor.transpose(bank[:, i, :], sigmoids[(c, half)][:, t * P : (t + 1) * P], ident_f32[:])
-                rows_out = result.tile([P, tiles, P], F32)
-                if piece < pieces_of(c) - 1:
-                    nc.vector.tensor_copy(out=rows_out[:], in_=bank[:])
+                group = [g for g in STORE_GROUPS if c in g][0]
+                first, place = group[0], c - group[0]
+                half, low = divmod(piece * tiles, TILES_PER_HALF)
+                if place == 0 and low == 0:
+                    rows_out[(first, half)] = wide.tile(
+                        [P, TILES_PER_HALF, len(group) * P], F32, name="rows_out%d" % len(group)
+                    )
+                mine = rows_out[(first, half)][:, low : low + tiles, place * P : (place + 1) * P]
+                if QUEUES == "by_chunk" and c < CHUNKS - 1:
+                    on_scalar = c % 2 == 1
                 else:
-                    nc.scalar.copy(out=rows_out[:], in_=bank[:])
+                    on_scalar = piece == pieces_of(c) - 1
+                if on_scalar:
+                    nc.scalar.copy(out=mine, in_=bank[:])
+                else:
+                    nc.vector.tensor_copy(out=mine, in_=bank[:])
+                queue = nc.scalar if on_scalar and QUEUES != "sync" else nc.sync
+                if place == len(group) - 1:
+                    queue.dma_start(
+                        out=out_view[:, tiles * piece : tiles * (piece + 1), first * P : (c + 1) * P],
+                        in_=rows_out[(first, half)][:, low : low + tiles, :],
+                    )
+
+        def turn_blocks_and_store(c):
+            turned = blocks.tile([P, ITEMS], F32, name="turned", align_bytes=64)
+            for half in range(HALVES):
+                nc.vector.transpose(out=turned[:, N_MOVE * half : N_MOVE * (half + 1)], in_=sigmoids[(c, half)][:])
+            for a in range(P // QUAD):
                 nc.sync.dma_start(
-                    out=out_view[:, tiles * piece : tiles * (piece + 1), c * P : (c + 1) * P], in_=rows_out[:]
+                    out=out[:, c * P + a * QUAD : c * P + (a + 1) * QUAD].rearrange("(b i) f -> i b f", i=QUAD),
+                    in_=turned[a * QUAD : (a + 1) * QUAD, :].rearrange("p (b f) -> p b f", f=QUAD),
                 )
 
         for j in range(TILES_PER_HALF):
             add_hops(j)
+            if j == GB_SPREAD_AT and j > 1:
+                spread_gamma_beta()
             if j >= 1:
                 quantise(j - 1, SELF)
             halve(j)
             flip(j)
             if j == 1:
-                spread_gamma_beta()
+                flip_gamma_beta()
+                if GB_SPREAD_AT == 1:
+                    spread_gamma_beta()
             if j >= 1:
                 quantise(j - 1, NEIGH)
+        for j in range(TILES_PER_HALF - 1):
+            for c in range(STREAMED):
+                multiply_tile(c, j)
         quantise(TILES_PER_HALF - 1, SELF)
+        if SEAM_FILL:
+            add_hops(TILES_PER_HALF)
         quantise(TILES_PER_HALF - 1, NEIGH)
+        for c in range(STREAMED):
+            multiply_tile(c, TILES_PER_HALF - 1)
+        early_done = []
+        measured = []
+        for c in range(STREAMED):
+            early_done.append(c)
         for i in range(TILES_PER_HALF):
             j = TILES_PER_HALF + i
-            multiply(i, 0)
-            add_hops(j)
-            order_self(j)
+            if i in EARLY_STEPS:
+                multiply(len(early_done), 0)
+                early_done.append(len(early_done))
+            if not (SEAM_FILL and i == 0):
+                add_hops(j)
+            if j in ORDER_SELF_TILES:
+                order_self(j)
             halve(j)
             flip(j)
             if i >= 1:
                 quantise(j - 1, SELF)
                 quantise(j - 1, NEIGH)
-            measure(i, 0)
-        for c in range(TILES_PER_HALF, EARLY_CHUNKS):
+            if len(measured) < len(early_done) and not DEFER_STATS:
+                c = len(measured)
+                measure(c, 0)
+                measured.append(c)
+                if c in PARKED:
+                    park(c)
+        for c in range(len(early_done), EARLY_CHUNKS):
             multiply(c, 0)
+        if DEFER_STATS == "weave":
+            for c in range(WEAVE_AHEAD):
+                measure(c, 0)
+                measured.append(c)
         quantise(ITEM_TILES - 1, SELF)
         quantise(ITEM_TILES - 1, NEIGH)
-        for c in range(TILES_PER_HALF, EARLY_CHUNKS):
-            measure(c, 0)
-        for c in range(TILES_PER_HALF, EARLY_CHUNKS):
-            park(c)
+        if DEFER_STATS != "weave":
+            for c in range(len(measured), EARLY_CHUNKS):
+                measure(c, 0)
+                measured.append(c)
+                if c in PARKED:
+                    park(c)
+        if EPS_IN_STATS:
+            lift(0, len(measured))
         def last_back(c):
             return c - (LAG_SHORT_STEPS if c < EARLY_CHUNKS else LAG_LONG_STEPS)
 
@@ -310,16 +453,33 @@ def tile_dogtaitujuanji_pb_kernel(
                 multiply(c, 0)
                 measure(c, 0)
                 finish_normalise(c - 1)
+                if EPS_IN_STATS:
+                    lift(c, c + 1)
             if c < CHUNKS:
                 multiply(c, 1)
                 measure(c, 1)
-            if 1 <= c < EARLY_CHUNKS or c == CHUNKS:
+            if (1 <= c < EARLY_CHUNKS or c == CHUNKS) and not AGGR_FIRST:
                 finish_normalise(c - 1)
             if c < CHUNKS:
                 aggregate(c)
+                if EPS_IN_STATS:
+                    power(c)
+            if (1 <= c < EARLY_CHUNKS or c == CHUNKS) and AGGR_FIRST:
+                finish_normalise(c - 1)
+            if len(measured) < EARLY_CHUNKS:
+                m = len(measured)
+                measure(m, 0)
+                measured.append(m)
+                if m in PARKED:
+                    park(m)
+                if EPS_IN_STATS:
+                    lift(m, m + 1)
             if c == CHUNKS - 1:
                 take_power(c)
             for b in range(max(0, last_back(c - 1) + 1), min(CHUNKS - 1, last_back(c)) + 1):
-                flip_back_and_store(b)
+                if b in VIA_BLOCKS:
+                    turn_blocks_and_store(b)
+                else:
+                    flip_back_and_store(b)
             if c < CHUNKS - 1:
                 take_power(c)

@@ -65,7 +65,7 @@ def tile_dogtaitujuanji_pb_kernel(
         small = ctx.enter_context(tc.tile_pool(name="small", bufs=4))
         result = ctx.enter_context(tc.tile_pool(name="result", bufs=8))
         blocks = ctx.enter_context(tc.tile_pool(name="blocks", bufs=2))
-        wide = ctx.enter_context(tc.tile_pool(name="wide", bufs=4))
+        wide = ctx.enter_context(tc.tile_pool(name="wide", bufs=8))
         psum = ctx.enter_context(tc.psum_pool(name="psum", bufs=8))
 
         gb_rows = keep.tile([P, P], BF16)

@@ -37,6 +37,9 @@ LAG_LONG_STEPS = 2
 HALVE_ON_SCALAR = False
 ORDER_SELF_TILES = (4, 5, 6, 7)
 SEAM_FILL = False
+VECTOR_COPY_TILES = ()
+SELF_FIRST = False
+OPEN0_PER_TILE = (2, 1, 1, 0)
 EPS_IN_STATS = True
 AGGR_FIRST = True
 QUAD = 32
@@ -44,9 +47,12 @@ VIA_BLOCKS = ()
 QUEUES = "sync"
 EARLY_STEPS = (0, 1, 2, 3)
 DEFER_STATS = False
+FINE_CHUNKS = (7,)
+MEASURE_IN_PHASE2 = 8
+MEASURE_AT_SEAM = 8
 WEAVE_AHEAD = 1
 STORE_GROUPS = ((0,), (1,), (2,), (3,), (4,), (5,), (6,), (7,))
-GB_SPREAD_AT = 1
+GB_SPREAD_AT = 2
 
 FLOPS = 2 * ITEMS * (2 * FEATS) * OUTS
 
@@ -80,6 +86,8 @@ def tile_dogtaitujuanji_pb_kernel(
 
         h_tiles = {}
         w_words = {}
+        self_views = {}
+        hop_views = {}
 
         def load_scales(src):
             by_row = scales_in[src].rearrange("g q n -> q g n")
@@ -91,6 +99,8 @@ def tile_dogtaitujuanji_pb_kernel(
         def load_items(j):
             h_tiles[j] = keep.tile([P, 3, FEATS], BF16, name="h%d" % j)
             nc.sync.dma_start(out=h_tiles[j][:], in_=h_sage[j * P : (j + 1) * P, :, :])
+            self_views[j] = h_tiles[j][:, 0, :]
+            hop_views[j] = (h_tiles[j][:, 1, :], h_tiles[j][:, 2, :])
 
         def load_words(src, part):
             width = 2 * P * CHUNKS_PER_PART
@@ -100,14 +110,35 @@ def tile_dogtaitujuanji_pb_kernel(
                 in_=words_in[src].rearrange("g p b -> p g b")[:, :, part * width : (part + 1) * width].bitcast(I32),
             )
 
-        load_items(0)
-        load_items(1)
-        load_scales(SELF)
-        load_items(2)
-        load_items(3)
-        load_scales(NEIGH)
-        load_words(SELF, 0)
-        load_words(NEIGH, 0)
+        def load_self_pair(j):
+            pair = keep.tile([P, 2, FEATS], BF16, name="self%d" % j)
+            nc.sync.dma_start(out=pair[:], in_=h_sage[j * P : (j + 2) * P, 0, :].rearrange("(t p) f -> p t f", p=P))
+            self_views[j] = pair[:, 0, :]
+            self_views[j + 1] = pair[:, 1, :]
+
+        def load_hops(j):
+            hops = keep.tile([P, 2, FEATS], BF16, name="hops%d" % j)
+            nc.sync.dma_start(out=hops[:], in_=h_sage[j * P : (j + 1) * P, 1:3, :])
+            hop_views[j] = (hops[:, 0, :], hops[:, 1, :])
+
+        if SELF_FIRST:
+            load_self_pair(0)
+            load_self_pair(2)
+            load_scales(SELF)
+            load_words(SELF, 0)
+            for j in range(TILES_PER_HALF):
+                load_hops(j)
+            load_scales(NEIGH)
+            load_words(NEIGH, 0)
+        else:
+            load_items(0)
+            load_items(1)
+            load_scales(SELF)
+            load_items(2)
+            load_items(3)
+            load_scales(NEIGH)
+            load_words(SELF, 0)
+            load_words(NEIGH, 0)
         for j in range(TILES_PER_HALF, ITEM_TILES + 1):
             if j == W1_BEFORE_TILE:
                 load_words(SELF, 1)
@@ -157,14 +188,14 @@ def tile_dogtaitujuanji_pb_kernel(
                 neigh_tiles[j] = stage.tile([P, FEATS], BF16, name="neigh")
                 nc.vector.tensor_tensor(
                     out=neigh_tiles[j][:].rearrange("p (u w e) -> p u w e", u=2, e=2),
-                    in0=h_tiles[j][:, 1, :].rearrange("p (w u e) -> p u w e", u=2, e=2),
-                    in1=h_tiles[j][:, 2, :].rearrange("p (w u e) -> p u w e", u=2, e=2),
+                    in0=hop_views[j][0].rearrange("p (w u e) -> p u w e", u=2, e=2),
+                    in1=hop_views[j][1].rearrange("p (w u e) -> p u w e", u=2, e=2),
                     op=ALU.add,
                 )
                 return
             hop_sums[j] = stage.tile([P, FEATS], BF16, name="hop_sum")
             nc.vector.tensor_tensor(
-                out=hop_sums[j][:], in0=h_tiles[j][:, 1, :], in1=h_tiles[j][:, 2, :], op=ALU.add
+                out=hop_sums[j][:], in0=hop_views[j][0], in1=hop_views[j][1], op=ALU.add
             )
 
         def halve(j):
@@ -185,13 +216,15 @@ def tile_dogtaitujuanji_pb_kernel(
             self_ordered[j] = stage.tile([P, FEATS], BF16, name="self_ordered")
             nc.vector.tensor_copy(
                 out=self_ordered[j][:].bitcast(F32).rearrange("p (u w) -> p u w", u=2),
-                in_=h_tiles[j][:, 0, :].bitcast(F32).rearrange("p (w u) -> p u w", u=2),
+                in_=self_views[j].bitcast(F32).rearrange("p (w u) -> p u w", u=2),
             )
 
-        def flip(j):
-            by_item = {SELF: self_ordered[j][:] if j in self_ordered else h_tiles[j][:, 0, :], NEIGH: neigh_tiles[j][:]}
-            for src in (SELF, NEIGH):
-                pairs = by_item[src].bitcast(F32)
+        def flip(j, srcs=(SELF, NEIGH)):
+            for src in srcs:
+                if src == SELF:
+                    pairs = (self_ordered[j][:] if j in self_ordered else self_views[j]).bitcast(F32)
+                else:
+                    pairs = neigh_tiles[j][:].bitcast(F32)
                 bank = psum.tile([P, GROUPS, 2, P], F32, tag="bank")
                 for g in range(GROUPS):
                     for u in range(2):
@@ -213,7 +246,8 @@ def tile_dogtaitujuanji_pb_kernel(
                             scale=0.5,
                         )
                     continue
-                nc.scalar.copy(
+                mover = nc.vector.tensor_copy if (src == NEIGH and j in VECTOR_COPY_TILES) else nc.scalar.copy
+                mover(
                     out=grouped[(j, src)][:]
                     .rearrange("p g i t -> p (g i t)")
                     .bitcast(F32)
@@ -230,12 +264,18 @@ def tile_dogtaitujuanji_pb_kernel(
                 )
 
         sums = {}
+        opened = []
         stats = keep.tile([P, CHUNKS, HALVES, 6], F32)
         passes = [(src, g) for src in (SELF, NEIGH) for g in range(GROUPS)]
 
-        def multiply(c, half):
-            sums[(c, half)] = psum.tile([P, N_MOVE], F32, tag="bank", name="sums")
+        def multiply(c, half, part=None):
+            if part is None and half == 0 and c in opened:
+                part = NEIGH
+            if part != NEIGH:
+                sums[(c, half)] = psum.tile([P, N_MOVE], F32, tag="bank", name="sums")
             for n, (src, g) in enumerate(passes):
+                if part is not None and src != part:
+                    continue
                 nc.tensor.matmul_mx(
                     out=sums[(c, half)][:],
                     lhsT=w_words[(src, c // CHUNKS_PER_PART)][
@@ -313,7 +353,7 @@ def tile_dogtaitujuanji_pb_kernel(
             )
 
         def pieces_of(c):
-            return 2 * HALVES if c == CHUNKS - 1 else HALVES
+            return 2 * HALVES if c in FINE_CHUNKS else HALVES
 
         def finish_normalise(c):
             affine = small.tile([P, 2], F32)
@@ -382,29 +422,54 @@ def tile_dogtaitujuanji_pb_kernel(
                     in_=turned[a * QUAD : (a + 1) * QUAD, :].rearrange("p (b f) -> p b f", f=QUAD),
                 )
 
-        for j in range(TILES_PER_HALF):
-            add_hops(j)
-            if j == GB_SPREAD_AT and j > 1:
-                spread_gamma_beta()
-            if j >= 1:
-                quantise(j - 1, SELF)
-            halve(j)
-            flip(j)
-            if j == 1:
-                flip_gamma_beta()
-                if GB_SPREAD_AT == 1:
+        if SELF_FIRST:
+            for j in range(TILES_PER_HALF):
+                flip(j, (SELF,))
+                if j >= 1:
+                    quantise(j - 1, SELF)
+            flip_gamma_beta()
+            quantise(TILES_PER_HALF - 1, SELF)
+            spread_gamma_beta()
+            add_hops(0)
+            for j in range(TILES_PER_HALF):
+                if j + 1 < TILES_PER_HALF:
+                    add_hops(j + 1)
+                halve(j)
+                for n in range(OPEN0_PER_TILE[j]):
+                    multiply(len(opened), 0, SELF)
+                    opened.append(len(opened))
+                flip(j, (NEIGH,))
+                if j >= 1:
+                    quantise(j - 1, NEIGH)
+            if SEAM_FILL:
+                add_hops(TILES_PER_HALF)
+            quantise(TILES_PER_HALF - 1, NEIGH)
+        else:
+            for j in range(TILES_PER_HALF):
+                if j in ORDER_SELF_TILES:
+                    order_self(j)
+                add_hops(j)
+                if j == GB_SPREAD_AT and j > 1:
                     spread_gamma_beta()
-            if j >= 1:
-                quantise(j - 1, NEIGH)
-        for j in range(TILES_PER_HALF - 1):
+                if j >= 1:
+                    quantise(j - 1, SELF)
+                halve(j)
+                flip(j)
+                if j == 1:
+                    flip_gamma_beta()
+                    if GB_SPREAD_AT == 1:
+                        spread_gamma_beta()
+                if j >= 1:
+                    quantise(j - 1, NEIGH)
+            for j in range(TILES_PER_HALF - 1):
+                for c in range(STREAMED):
+                    multiply_tile(c, j)
+            quantise(TILES_PER_HALF - 1, SELF)
+            if SEAM_FILL:
+                add_hops(TILES_PER_HALF)
+            quantise(TILES_PER_HALF - 1, NEIGH)
             for c in range(STREAMED):
-                multiply_tile(c, j)
-        quantise(TILES_PER_HALF - 1, SELF)
-        if SEAM_FILL:
-            add_hops(TILES_PER_HALF)
-        quantise(TILES_PER_HALF - 1, NEIGH)
-        for c in range(STREAMED):
-            multiply_tile(c, TILES_PER_HALF - 1)
+                multiply_tile(c, TILES_PER_HALF - 1)
         early_done = []
         measured = []
         for c in range(STREAMED):
@@ -423,7 +488,7 @@ def tile_dogtaitujuanji_pb_kernel(
             if i >= 1:
                 quantise(j - 1, SELF)
                 quantise(j - 1, NEIGH)
-            if len(measured) < len(early_done) and not DEFER_STATS:
+            if len(measured) < min(len(early_done), MEASURE_IN_PHASE2) and not DEFER_STATS:
                 c = len(measured)
                 measure(c, 0)
                 measured.append(c)
@@ -438,7 +503,7 @@ def tile_dogtaitujuanji_pb_kernel(
         quantise(ITEM_TILES - 1, SELF)
         quantise(ITEM_TILES - 1, NEIGH)
         if DEFER_STATS != "weave":
-            for c in range(len(measured), EARLY_CHUNKS):
+            for c in range(len(measured), min(EARLY_CHUNKS, MEASURE_AT_SEAM)):
                 measure(c, 0)
                 measured.append(c)
                 if c in PARKED:

from contextlib import ExitStack

import concourse.mybir as mybir
from concourse.masks import make_identity

F32 = mybir.dt.float32
BF16 = mybir.dt.bfloat16
U8 = mybir.dt.uint8
U32 = mybir.dt.uint32
I32 = mybir.dt.int32
FP8X4 = mybir.dt.float8_e4m3fn_x4
FP4X4 = mybir.dt.float4_e2m1fn_x4
ALU = mybir.AluOpType
ACT = mybir.ActivationFunctionType

P = 128
ITEMS = 1024
FEATS = 1024
OUTS = 1024
K_PASS = 512
GROUPS = FEATS // K_PASS
ITEM_TILES = ITEMS // P
N_MOVE = 512
HALVES = ITEMS // N_MOVE
TILES_PER_HALF = N_MOVE // P
CHUNKS = OUTS // P
BN_EPS = 1e-5
SELF, NEIGH = 0, 1
STREAMED = 0
PARKED = (4,)
W1_BEFORE_TILE = 8
EARLY_CHUNKS = 5
W_PARTS = 2
CHUNKS_PER_PART = CHUNKS // W_PARTS
LAG_SHORT_STEPS = 3
LAG_LONG_STEPS = 2
HALVE_ON_SCALAR = False
ORDER_SELF_TILES = (4, 5, 6, 7)
SEAM_FILL = False
VECTOR_COPY_TILES = ()
SELF_FIRST = False
OPEN0_PER_TILE = (2, 1, 1, 0)
EPS_IN_STATS = True
AGGR_FIRST = True
QUAD = 32
VIA_BLOCKS = ()
QUEUES = "sync"
EARLY_STEPS = (0, 1, 2, 3)
DEFER_STATS = False
FINE_CHUNKS = (7,)
MEASURE_IN_PHASE2 = 8
MEASURE_AT_SEAM = 8
WEAVE_AHEAD = 1
STORE_GROUPS = ((0,), (1,), (2,), (3,), (4,), (5,), (6,), (7,))
GB_SPREAD_AT = 2

FLOPS = 2 * ITEMS * (2 * FEATS) * OUTS


def tile_dogtaitujuanji_pb_kernel(
    tc, h_sage, w1b_words, w1b_scales, w2b_words, w2b_scales, gamma, beta, out
):
    nc = tc.nc
    words_in = {SELF: w2b_words, NEIGH: w1b_words}
    scales_in = {SELF: w2b_scales, NEIGH: w1b_scales}

    with ExitStack() as ctx:
        ctx.enter_context(tc.manual_schedule())
        keep = ctx.enter_context(tc.tile_pool(name="keep", bufs=1))
        stage = ctx.enter_context(tc.tile_pool(name="stage", bufs=4))
        small = ctx.enter_context(tc.tile_pool(name="small", bufs=4))
        result = ctx.enter_context(tc.tile_pool(name="result", bufs=8))
        blocks = ctx.enter_context(tc.tile_pool(name="blocks", bufs=2))
        wide = ctx.enter_context(tc.tile_pool(name="wide", bufs=8))
        psum = ctx.enter_context(tc.psum_pool(name="psum", bufs=8))

        gb_rows = keep.tile([P, P], BF16)
        nc.vector.memset(gb_rows[:], 0.0)
        w_planes = keep.tile([P, 2, GROUPS, OUTS], U8, align_bytes=64)
        nc.vector.memset(w_planes[:].rearrange("p s g n -> p (s g n)").bitcast(I32), 0)
        warm = keep.tile([P, 1], F32)
        nc.vector.memset(warm[:], 0.0)

        nc.scalar.dma_start(out=gb_rows[0:CHUNKS, :], in_=gamma.rearrange("(c f) -> c f", f=P))
        nc.scalar.dma_start(out=gb_rows[CHUNKS : 2 * CHUNKS, :], in_=beta.rearrange("(c f) -> c f", f=P))

        h_tiles = {}
        w_words = {}
        self_views = {}
        hop_views = {}

        def load_scales(src):
            by_row = scales_in[src].rearrange("g q n -> q g n")
            for r in range(4):
                nc.sync.dma_start(
                    out=w_planes[r:P:32, src, :, :].bitcast(I32), in_=by_row[r:16:4, :, :].bitcast(I32)
                )

        def load_items(j):
            h_tiles[j] = keep.tile([P, 3, FEATS], BF16, name="h%d" % j)
            nc.sync.dma_start(out=h_tiles[j][:], in_=h_sage[j * P : (j + 1) * P, :, :])
            self_views[j] = h_tiles[j][:, 0, :]
            hop_views[j] = (h_tiles[j][:, 1, :], h_tiles[j][:, 2, :])

        def load_words(src, part):
            width = 2 * P * CHUNKS_PER_PART
            w_words[(src, part)] = keep.tile([P, GROUPS, width], U8, name="w%d_%d" % (src, part), align_bytes=64)
            nc.sync.dma_start(
                out=w_words[(src, part)][:].bitcast(I32),
                in_=words_in[src].rearrange("g p b -> p g b")[:, :, part * width : (part + 1) * width].bitcast(I32),
            )

        def load_self_pair(j):
            pair = keep.tile([P, 2, FEATS], BF16, name="self%d" % j)
            nc.sync.dma_start(out=pair[:], in_=h_sage[j * P : (j + 2) * P, 0, :].rearrange("(t p) f -> p t f", p=P))
            self_views[j] = pair[:, 0, :]
            self_views[j + 1] = pair[:, 1, :]

        def load_hops(j):
            hops = keep.tile([P, 2, FEATS], BF16, name="hops%d" % j)
            nc.sync.dma_start(out=hops[:], in_=h_sage[j * P : (j + 1) * P, 1:3, :])
            hop_views[j] = (hops[:, 0, :], hops[:, 1, :])

        if SELF_FIRST:
            load_self_pair(0)
            load_self_pair(2)
            load_scales(SELF)
            load_words(SELF, 0)
            for j in range(TILES_PER_HALF):
                load_hops(j)
            load_scales(NEIGH)
            load_words(NEIGH, 0)
        else:
            load_items(0)
            load_items(1)
            load_scales(SELF)
            load_items(2)
            load_items(3)
            load_scales(NEIGH)
            load_words(SELF, 0)
            load_words(NEIGH, 0)
        for j in range(TILES_PER_HALF, ITEM_TILES + 1):
            if j == W1_BEFORE_TILE:
                load_words(SELF, 1)
                load_words(NEIGH, 1)
            if j < ITEM_TILES:
                load_items(j)

        ident_f32 = keep.tile([P, P], F32)
        make_identity(nc, ident_f32[:])
        ident_bf16 = keep.tile([P, P], BF16)
        make_identity(nc, ident_bf16[:])
        neg_half = keep.tile([P, 1], F32)
        nc.gpsimd.memset(neg_half[:], -0.5)
        nc.scalar.activation(out=warm[:], in_=warm[:], func=ACT.Sigmoid)

        factors = keep.tile([P, CHUNKS, 2], F32)
        addends = keep.tile([P, CHUNKS, 2], F32)
        nc.vector.memset(addends[:], 0.0)
        neg_gamma = keep.tile([P, CHUNKS], F32)

        gb_banks = []

        def flip_gamma_beta():
            gb_banks.append(psum.tile([P, P], BF16, tag="bank", name="gb_bank"))
            nc.tensor.transpose(gb_banks[0][:], gb_rows[:], ident_bf16[:])

        def spread_gamma_beta():
            gb_bank = gb_banks[0]
            nc.vector.tensor_copy(out=factors[:, :, 0], in_=gb_bank[:, 0:CHUNKS])
            nc.vector.tensor_copy(out=addends[:, :, 1], in_=gb_bank[:, CHUNKS : 2 * CHUNKS])
            nc.vector.tensor_scalar(
                out=neg_gamma[:], in0=gb_bank[:, 0:CHUNKS], scalar1=-1.0, scalar2=None, op0=ALU.mult
            )

        x_codes = {}
        x_planes = {}
        for src in (SELF, NEIGH):
            x_codes[src] = keep.tile([P, GROUPS, ITEMS], U32, name="x_codes%d" % src, align_bytes=64)
            x_planes[src] = keep.tile([P, GROUPS, ITEMS], U8, name="x_planes%d" % src, align_bytes=64)
        neigh_tiles = {}
        grouped = {}

        hop_sums = {}

        def add_hops(j):
            if HALVE_ON_SCALAR:
                neigh_tiles[j] = stage.tile([P, FEATS], BF16, name="neigh")
                nc.vector.tensor_tensor(
                    out=neigh_tiles[j][:].rearrange("p (u w e) -> p u w e", u=2, e=2),
                    in0=hop_views[j][0].rearrange("p (w u e) -> p u w e", u=2, e=2),
                    in1=hop_views[j][1].rearrange("p (w u e) -> p u w e", u=2, e=2),
                    op=ALU.add,
                )
                return
            hop_sums[j] = stage.tile([P, FEATS], BF16, name="hop_sum")
            nc.vector.tensor_tensor(
                out=hop_sums[j][:], in0=hop_views[j][0], in1=hop_views[j][1], op=ALU.add
            )

        def halve(j):
            if HALVE_ON_SCALAR:
                return
            neigh_tiles[j] = stage.tile([P, FEATS], BF16, name="neigh")
            nc.vector.tensor_scalar(
                out=neigh_tiles[j][:].rearrange("p (u w e) -> p u w e", u=2, e=2),
                in0=hop_sums[j][:].rearrange("p (w u e) -> p u w e", u=2, e=2),
                scalar1=0.5,
                scalar2=None,
                op0=ALU.mult,
            )

        self_ordered = {}

        def order_self(j):
            self_ordered[j] = stage.tile([P, FEATS], BF16, name="self_ordered")
            nc.vector.tensor_copy(
                out=self_ordered[j][:].bitcast(F32).rearrange("p (u w) -> p u w", u=2),
                in_=self_views[j].bitcast(F32).rearrange("p (w u) -> p u w", u=2),
            )

        def flip(j, srcs=(SELF, NEIGH)):
            for src in srcs:
                if src == SELF:
                    pairs = (self_ordered[j][:] if j in self_ordered else self_views[j]).bitcast(F32)
                else:
                    pairs = neigh_tiles[j][:].bitcast(F32)
                bank = psum.tile([P, GROUPS, 2, P], F32, tag="bank")
                for g in range(GROUPS):
                    for u in range(2):
                        if src == SELF and j not in self_ordered:
                            words = pairs[:, 256 * g + u : 256 * (g + 1) : 2]
                        else:
                            words = pairs[:, 256 * u + P * g : 256 * u + P * (g + 1)]
                        nc.tensor.transpose(bank[:, g, u, :], words, ident_f32[:])
                grouped[(j, src)] = stage.tile([P, GROUPS, P, 4], BF16, name="grouped%d" % src, align_bytes=64)
                if src == NEIGH and HALVE_ON_SCALAR:
                    for g in range(GROUPS):
                        nc.scalar.activation(
                            out=grouped[(j, src)][:, g, :, :].rearrange("p i (u e) -> p i u e", e=2),
                            in_=bank[:, g, :, :]
                            .rearrange("p u i -> p (u i)")
                            .bitcast(BF16)
                            .rearrange("p (u i e) -> p i u e", u=2, e=2),
                            func=ACT.Copy,
                            scale=0.5,
                        )
                    continue
                mover = nc.vector.tensor_copy if (src == NEIGH and j in VECTOR_COPY_TILES) else nc.scalar.copy
                mover(
                    out=grouped[(j, src)][:]
                    .rearrange("p g i t -> p (g i t)")
                    .bitcast(F32)
                    .rearrange("p (g i u) -> p g i u", g=GROUPS, u=2),
                    in_=bank[:].rearrange("p g u i -> p g i u"),
                )

        def quantise(j, src):
            for g in range(GROUPS):
                nc.vector.quantize_mx(
                    out=x_codes[src][:, g, j * P : (j + 1) * P].bitcast(FP8X4),
                    scales=x_planes[src][:, g, j * P : (j + 1) * P],
                    in_=grouped[(j, src)][:, g, :, :].rearrange("p i t -> p (i t)"),
                )

        sums = {}
        opened = []
        stats = keep.tile([P, CHUNKS, HALVES, 6], F32)
        passes = [(src, g) for src in (SELF, NEIGH) for g in range(GROUPS)]

        def multiply(c, half, part=None):
            if part is None and half == 0 and c in opened:
                part = NEIGH
            if part != NEIGH:
                sums[(c, half)] = psum.tile([P, N_MOVE], F32, tag="bank", name="sums")
            for n, (src, g) in enumerate(passes):
                if part is not None and src != part:
                    continue
                nc.tensor.matmul_mx(
                    out=sums[(c, half)][:],
                    lhsT=w_words[(src, c // CHUNKS_PER_PART)][
                        :, g, 2 * P * (c % CHUNKS_PER_PART) : 2 * P * (c % CHUNKS_PER_PART + 1)
                    ].bitcast(FP4X4),
                    lhsT_scale=w_planes[:, src, g, P * c : P * (c + 1)],
                    rhs=x_codes[src][:, g, N_MOVE * half : N_MOVE * (half + 1)].bitcast(FP8X4),
                    rhs_scale=x_planes[src][:, g, N_MOVE * half : N_MOVE * (half + 1)],
                    start=(n == 0),
                    stop=(n == len(passes) - 1),
                )

        def multiply_tile(c, j):
            if j == 0:
                sums[(c, 0)] = psum.tile([P, N_MOVE], F32, tag="bank", name="sums")
            for n, (src, g) in enumerate(passes):
                nc.tensor.matmul_mx(
                    out=sums[(c, 0)][:, j * P : (j + 1) * P],
                    lhsT=w_words[(src, c // CHUNKS_PER_PART)][
                        :, g, 2 * P * (c % CHUNKS_PER_PART) : 2 * P * (c % CHUNKS_PER_PART + 1)
                    ].bitcast(FP4X4),
                    lhsT_scale=w_planes[:, src, g, P * c : P * (c + 1)],
                    rhs=x_codes[src][:, g, j * P : (j + 1) * P].bitcast(FP8X4),
                    rhs_scale=x_planes[src][:, g, j * P : (j + 1) * P],
                    start=(n == 0),
                    stop=(n == len(passes) - 1),
                )

        def measure(c, half):
            nc.vector.bn_stats(out=stats[:, c, half, :], in_=sums[(c, half)][:])

        mean_var = {}
        rstd = {}
        sigmoids = {}

        def park(c):
            parked = keep.tile([P, N_MOVE], F32, name="parked%d" % c)
            nc.scalar.copy(out=parked[:], in_=sums[(c, 0)][:])
            sums[(c, 0)] = parked

        def aggregate(c):
            mean_var[c] = small.tile([P, 2], F32, name="mean_var")
            nc.vector.bn_aggr(out=mean_var[c][:], in_=stats[:, c, :, :].rearrange("p h s -> p (h s)"))

        def lift(first, last):
            nc.vector.tensor_scalar(
                out=stats[:, first:last, 0, 2:3],
                in0=stats[:, first:last, 0, 2:3],
                scalar1=ITEMS * BN_EPS,
                scalar2=None,
                op0=ALU.add,
            )

        def power(c):
            rstd[c] = small.tile([P, 1], F32, name="rstd")
            nc.gpsimd.tensor_tensor(out=rstd[c][:], in0=mean_var[c][:, 1:2], in1=neg_half[:], op=ALU.pow)

        def scale_mean(c):
            nc.vector.tensor_tensor(
                out=factors[:, c, 1:2], in0=mean_var[c][:, 0:1], in1=neg_gamma[:, c : c + 1], op=ALU.mult
            )

        def take_power(c):
            if EPS_IN_STATS:
                scale_mean(c)
                return
            var_eps = small.tile([P, 1], F32)
            nc.vector.tensor_scalar(
                out=var_eps[:], in0=mean_var[c][:, 1:2], scalar1=BN_EPS, scalar2=None, op0=ALU.add
            )
            rstd[c] = small.tile([P, 1], F32, name="rstd")
            nc.gpsimd.tensor_tensor(out=rstd[c][:], in0=var_eps[:], in1=neg_half[:], op=ALU.pow)
            nc.vector.tensor_tensor(
                out=factors[:, c, 1:2], in0=mean_var[c][:, 0:1], in1=neg_gamma[:, c : c + 1], op=ALU.mult
            )

        def pieces_of(c):
            return 2 * HALVES if c in FINE_CHUNKS else HALVES

        def finish_normalise(c):
            affine = small.tile([P, 2], F32)
            nc.vector.scalar_tensor_tensor(
                out=affine[:],
                in0=factors[:, c, :],
                scalar=rstd[c][:],
                in1=addends[:, c, :],
                op0=ALU.mult,
                op1=ALU.add,
            )
            for half in range(HALVES):
                sigmoids[(c, half)] = result.tile([P, N_MOVE], F32, name="sigmoid", align_bytes=64)
            width = ITEMS // pieces_of(c)
            for piece in range(pieces_of(c)):
                half, low = divmod(piece * width, N_MOVE)
                nc.scalar.activation(
                    out=sigmoids[(c, half)][:, low : low + width],
                    in_=sums[(c, half)][:, low : low + width],
                    func=ACT.Sigmoid,
                    bias=affine[:, 1:2],
                    scale=affine[:, 0:1],
                )

        out_view = out.rearrange("(j p) f -> p j f", p=P)

        rows_out = {}

        def flip_back_and_store(c):
            tiles = ITEM_TILES // pieces_of(c)
            for piece in range(pieces_of(c)):
                bank = psum.tile([P, tiles, P], F32, tag="bank")
                for i in range(tiles):
                    half, t = divmod(piece * tiles + i, TILES_PER_HALF)
                    nc.tensor.transpose(bank[:, i, :], sigmoids[(c, half)][:, t * P : (t + 1) * P], ident_f32[:])
                group = [g for g in STORE_GROUPS if c in g][0]
                first, place = group[0], c - group[0]
                half, low = divmod(piece * tiles, TILES_PER_HALF)
                if place == 0 and low == 0:
                    rows_out[(first, half)] = wide.tile(
                        [P, TILES_PER_HALF, len(group) * P], F32, name="rows_out%d" % len(group)
                    )
                mine = rows_out[(first, half)][:, low : low + tiles, place * P : (place + 1) * P]
                if QUEUES == "by_chunk" and c < CHUNKS - 1:
                    on_scalar = c % 2 == 1
                else:
                    on_scalar = piece == pieces_of(c) - 1
                if on_scalar:
                    nc.scalar.copy(out=mine, in_=bank[:])
                else:
                    nc.vector.tensor_copy(out=mine, in_=bank[:])
                queue = nc.scalar if on_scalar and QUEUES != "sync" else nc.sync
                if place == len(group) - 1:
                    queue.dma_start(
                        out=out_view[:, tiles * piece : tiles * (piece + 1), first * P : (c + 1) * P],
                        in_=rows_out[(first, half)][:, low : low + tiles, :],
                    )

        def turn_blocks_and_store(c):
            turned = blocks.tile([P, ITEMS], F32, name="turned", align_bytes=64)
            for half in range(HALVES):
                nc.vector.transpose(out=turned[:, N_MOVE * half : N_MOVE * (half + 1)], in_=sigmoids[(c, half)][:])
            for a in range(P // QUAD):
                nc.sync.dma_start(
                    out=out[:, c * P + a * QUAD : c * P + (a + 1) * QUAD].rearrange("(b i) f -> i b f", i=QUAD),
                    in_=turned[a * QUAD : (a + 1) * QUAD, :].rearrange("p (b f) -> p b f", f=QUAD),
                )

        if SELF_FIRST:
            for j in range(TILES_PER_HALF):
                flip(j, (SELF,))
                if j >= 1:
                    quantise(j - 1, SELF)
            flip_gamma_beta()
            quantise(TILES_PER_HALF - 1, SELF)
            spread_gamma_beta()
            add_hops(0)
            for j in range(TILES_PER_HALF):
                if j + 1 < TILES_PER_HALF:
                    add_hops(j + 1)
                halve(j)
                for n in range(OPEN0_PER_TILE[j]):
                    multiply(len(opened), 0, SELF)
                    opened.append(len(opened))
                flip(j, (NEIGH,))
                if j >= 1:
                    quantise(j - 1, NEIGH)
            if SEAM_FILL:
                add_hops(TILES_PER_HALF)
            quantise(TILES_PER_HALF - 1, NEIGH)
        else:
            for j in range(TILES_PER_HALF):
                if j in ORDER_SELF_TILES:
                    order_self(j)
                add_hops(j)
                if j == GB_SPREAD_AT and j > 1:
                    spread_gamma_beta()
                if j >= 1:
                    quantise(j - 1, SELF)
                halve(j)
                flip(j)
                if j == 1:
                    flip_gamma_beta()
                    if GB_SPREAD_AT == 1:
                        spread_gamma_beta()
                if j >= 1:
                    quantise(j - 1, NEIGH)
            for j in range(TILES_PER_HALF - 1):
                for c in range(STREAMED):
                    multiply_tile(c, j)
            quantise(TILES_PER_HALF - 1, SELF)
            if SEAM_FILL:
                add_hops(TILES_PER_HALF)
            quantise(TILES_PER_HALF - 1, NEIGH)
            for c in range(STREAMED):
                multiply_tile(c, TILES_PER_HALF - 1)
        early_done = []
        measured = []
        for c in range(STREAMED):
            early_done.append(c)
        for i in range(TILES_PER_HALF):
            j = TILES_PER_HALF + i
            if i in EARLY_STEPS:
                multiply(len(early_done), 0)
                early_done.append(len(early_done))
            if not (SEAM_FILL and i == 0):
                add_hops(j)
            if j in ORDER_SELF_TILES:
                order_self(j)
            halve(j)
            flip(j)
            if i >= 1:
                quantise(j - 1, SELF)
                quantise(j - 1, NEIGH)
            if len(measured) < min(len(early_done), MEASURE_IN_PHASE2) and not DEFER_STATS:
                c = len(measured)
                measure(c, 0)
                measured.append(c)
                if c in PARKED:
                    park(c)
        for c in range(len(early_done), EARLY_CHUNKS):
            multiply(c, 0)
        if DEFER_STATS == "weave":
            for c in range(WEAVE_AHEAD):
                measure(c, 0)
                measured.append(c)
        quantise(ITEM_TILES - 1, SELF)
        quantise(ITEM_TILES - 1, NEIGH)
        if DEFER_STATS != "weave":
            for c in range(len(measured), min(EARLY_CHUNKS, MEASURE_AT_SEAM)):
                measure(c, 0)
                measured.append(c)
                if c in PARKED:
                    park(c)
        if EPS_IN_STATS:
            lift(0, len(measured))
        def last_back(c):
            return c - (LAG_SHORT_STEPS if c < EARLY_CHUNKS else LAG_LONG_STEPS)

        for c in range(CHUNKS + LAG_LONG_STEPS):
            if EARLY_CHUNKS <= c < CHUNKS:
                multiply(c, 0)
                measure(c, 0)
                finish_normalise(c - 1)
                if EPS_IN_STATS:
                    lift(c, c + 1)
            if c < CHUNKS:
                multiply(c, 1)
                measure(c, 1)
            if (1 <= c < EARLY_CHUNKS or c == CHUNKS) and not AGGR_FIRST:
                finish_normalise(c - 1)
            if c < CHUNKS:
                aggregate(c)
                if EPS_IN_STATS:
                    power(c)
            if (1 <= c < EARLY_CHUNKS or c == CHUNKS) and AGGR_FIRST:
                finish_normalise(c - 1)
            if len(measured) < EARLY_CHUNKS:
                m = len(measured)
                measure(m, 0)
                measured.append(m)
                if m in PARKED:
                    park(m)
                if EPS_IN_STATS:
                    lift(m, m + 1)
            if c == CHUNKS - 1:
                take_power(c)
            for b in range(max(0, last_back(c - 1) + 1), min(CHUNKS - 1, last_back(c)) + 1):
                if b in VIA_BLOCKS:
                    turn_blocks_and_store(b)
                else:
                    flip_back_and_store(b)
            if c < CHUNKS - 1:
                take_power(c)
